import numpy as np
import ml_dtypes


def mxq(x, axis, fmt="e4m3"):
    dtype, down = {"e4m3": (ml_dtypes.float8_e4m3fn, 7), "e5m2": (ml_dtypes.float8_e5m2, 14)}[fmt]
    v = np.moveaxis(np.asarray(x, np.float32).astype(ml_dtypes.bfloat16).astype(np.float64), axis, -1)
    blocks = v.reshape(v.shape[:-1] + (-1, 32))
    amax = np.abs(blocks).max(-1, keepdims=True)
    byte = np.maximum(np.where(amax > 0, np.frexp(amax)[1] - 1 + 127, 0) - down, 1)
    scale = np.exp2(byte - 127.0)
    codes = (blocks / scale).astype(np.float32).astype(dtype).astype(np.float64)
    return np.moveaxis((codes * scale).reshape(v.shape), -1, axis)


WIDE = False


def mx_kscale(k):
    if not WIDE:
        return np.ones(k)
    levels = np.array([10, -10, 5, -5, 0])
    if k % 512:
        return np.exp2(np.random.permutation(np.resize(levels, k // 32))).repeat(32)
    a = np.empty((k // 512, 16))
    for p in range(k // 512):
        a[p, :8] = np.random.permutation(np.resize(levels, 8))
        for g in range(8):
            far = levels[np.abs(levels - a[p, g]) >= 10]
            a[p, g + 8] = far[np.random.randint(len(far))]
    return np.exp2(a.ravel()).repeat(32)


BF16 = ml_dtypes.bfloat16


def bf(x):
    return np.asarray(x, np.float32).astype(BF16)


def f64(x):
    return np.asarray(x).astype(np.float64)


B, J, I, O = 1024, 8, 512, 128
IN_CH = J * I
OUT_CH = J * O
NEIGHBOUR_LIST = [[j for j in (i - 1, i, i + 1) if 0 <= j < J] for i in range(J)]


def build_mask():
    mask = np.zeros((OUT_CH, IN_CH))
    for i, neigh in enumerate(NEIGHBOUR_LIST):
        mask[i * O:(i + 1) * O, neigh[0] * I:(neigh[-1] + 1) * I] = 1.0
    return mask


def setup_inputs():
    s = mx_kscale(IN_CH)
    keep = np.random.random((OUT_CH, IN_CH)) < 0.75
    return {"x": bf(np.random.standard_normal((B, IN_CH)) * s),
            "weight": bf(np.random.standard_normal((OUT_CH, IN_CH)) / np.sqrt(0.75 * 3 * I) / s[None, :]),
            "mask": bf(build_mask() * keep),
            "bias": bf(np.random.standard_normal(OUT_CH) * 0.5)}


def reference(x, weight, mask, bias):
    x2 = f64(x).reshape(x.shape[0], -1)
    w = f64(weight) * f64(mask)
    xq = mxq(x2, 1, "e4m3")
    cols = []
    for i, neigh in enumerate(NEIGHBOUR_LIST):
        lo, hi = neigh[0] * I, (neigh[-1] + 1) * I
        cols.append(xq[:, lo:hi] @ mxq(w[i * O:(i + 1) * O, lo:hi], 1, "e4m3").T)
    return np.concatenate(cols, axis=1) + f64(bias)

@@ -1,0 +1,211 @@
+from contextlib import ExitStack
+
+import concourse.mybir as mybir
+from concourse.masks import make_identity
+
+F32 = mybir.dt.float32
+BF16 = mybir.dt.bfloat16
+U32 = mybir.dt.uint32
+U8 = mybir.dt.uint8
+FP8X4 = mybir.dt.float8_e4m3fn_x4
+ADD = mybir.AluOpType.add
+MULT = mybir.AluOpType.mult
+
+P = 128
+B, J, I, O = 1024, 8, 512, 128
+NT = B // P
+NBLK = 3 * J - 2
+FLOPS = 2 * B * O * I * NBLK
+BYTES = 2 * B * J * I + 2 * 2 * NBLK * O * I + 2 * J * O + 4 * B * J * O
+
+NF = 4
+
+
+def neighbours(i):
+    return list(range(max(i - 1, 0), min(i + 2, J)))
+
+
+def tile_skeletonlinear_kernel(tc, x, weight, mask, bias, out):
+    nc = tc.nc
+    with ExitStack() as ctx:
+        const = ctx.enter_context(tc.tile_pool(name="const", bufs=1))
+        keep = ctx.enter_context(tc.tile_pool(name="keep", bufs=1))
+        xraw = ctx.enter_context(tc.tile_pool(name="xraw", bufs=4))
+        grp = ctx.enter_context(tc.tile_pool(name="grp", bufs=3))
+        psum_t = ctx.enter_context(tc.psum_pool(name="psum_t", bufs=4))
+        psum_a = ctx.enter_context(tc.psum_pool(name="psum_a", bufs=4))
+        ctx.enter_context(tc.manual_schedule())
+
+        x_view = x.rearrange("(t p) k -> p t k", p=P)
+        out_view = out.rearrange("(t p) o -> p t o", p=P)
+
+        ident = const.tile([P, P], F32, name="ident")
+        make_identity(nc, ident[:])
+        ones = const.tile([P, P], BF16, name="ones")
+        nc.vector.memset(ones[:], 1.0)
+        brow = const.tile([P, J * O], BF16, name="brow")
+        nc.vector.memset(brow[:], 0.0)
+        bias_bc = const.tile([P, J * O], F32, name="bias_bc")
+
+        xr = {}
+        wr = {}
+        mr = {}
+        gt = {}
+        xc = {}
+        xs = {}
+        wc = {}
+        ws = {}
+        accs = {}
+
+        def load_x(t):
+            xr[t] = xraw.tile([P, J * I], BF16, name="xr%d" % t, tag="xr")
+            nc.sync.dma_start(out=xr[t][:], in_=x_view[:, t, :])
+
+        def load_w(i):
+            ng = neighbours(i)
+            n = len(ng) * I
+            lo = ng[0] * I
+            wr[i] = keep.tile([P, n], BF16, name="wr%d" % i)
+            mr[i] = keep.tile([P, n], BF16, name="mr%d" % i)
+            nc.sync.dma_start(out=wr[i][:], in_=weight[i * O:(i + 1) * O, lo:lo + n])
+            nc.sync.dma_start(out=mr[i][:], in_=mask[i * O:(i + 1) * O, lo:lo + n])
+
+        def bias_spread():
+            for h in range(2):
+                pb = psum_a.tile([P, 512], F32, name="pb", tag="acc")
+                nc.tensor.matmul(out=pb[:], lhsT=ones[:], rhs=brow[:, 512 * h:512 * (h + 1)], start=True, stop=True)
+                nc.vector.tensor_copy(out=bias_bc[:, 512 * h:512 * (h + 1)], in_=pb[:])
+
+        def transpose_group(src32, nblk, g32, dve_banks):
+            for b0 in range(0, nblk, 2):
+                nb = min(2, nblk - b0)
+                tp = psum_t.tile([P, 2, 2, P], F32, name="tp", tag="tp")
+                for gg in range(nb):
+                    for u in range(2):
+                        c0 = 256 * (b0 + gg)
+                        nc.tensor.transpose(out=tp[:, gg, u, :], in_=src32[:, c0 + u:c0 + 256:2], identity=ident[:])
+                src = tp[:, 0:nb, :, :].rearrange("p g u r -> p g r u")
+                if b0 // 2 in dve_banks:
+                    nc.vector.tensor_copy(out=g32[:, b0:b0 + nb, :, :], in_=src)
+                else:
+                    nc.scalar.copy(out=g32[:, b0:b0 + nb, :, :], in_=src)
+
+        steps = [("x", t) for t in range(NF)] + [("w", i) for i in range(J)] + [("x", t) for t in range(NF, NT)]
+        N = len(steps)
+
+        def stage_mask(step):
+            kind, i = step
+            if kind == "w":
+                nc.vector.tensor_tensor(out=wr[i][:], in0=wr[i][:], in1=mr[i][:], op=MULT)
+
+        def stage_transpose(step):
+            kind, n = step
+            if kind == "x":
+                g = grp.tile([P, 4 * J * P], BF16, name="gx", tag="gx", align_bytes=64)
+                g32 = g[:].bitcast(F32).rearrange("p (g r u) -> p g r u", g=J, r=P, u=2)
+                transpose_group(xr[n][:].bitcast(F32), J, g32, [])
+            else:
+                g = grp.tile([P, 4 * 3 * P], BF16, name="gw", tag="gw", align_bytes=64)
+                g32 = g[:].bitcast(F32).rearrange("p (g r u) -> p g r u", g=3, r=P, u=2)
+                transpose_group(wr[n][:].bitcast(F32), len(neighbours(n)), g32, [])
+            gt[step] = g
+
+        def stage_quantise(step):
+            kind, n = step
+            g = gt[step]
+            if kind == "x":
+                xc[n] = keep.tile([P, J * P], U32, name="xc%d" % n, align_bytes=64)
+                xs[n] = keep.tile([P, J * P], U8, name="xs%d" % n, align_bytes=64)
+                for h in range(2):
+                    nc.vector.quantize_mx(
+                        out=xc[n][:, 512 * h:512 * (h + 1)].bitcast(FP8X4),
+                        scales=xs[n][:, 512 * h:512 * (h + 1)],
+                        in_=g[:, 2048 * h:2048 * (h + 1)],
+                    )
+            else:
+                nblk = len(neighbours(n))
+                wc[n] = keep.tile([P, 3 * P], U32, name="wc%d" % n, align_bytes=64)
+                ws[n] = keep.tile([P, 3 * P], U8, name="ws%d" % n, align_bytes=64)
+                for b0 in range(0, nblk, 2):
+                    nb = min(2, nblk - b0)
+                    nc.vector.quantize_mx(
+                        out=wc[n][:, P * b0:P * (b0 + nb)].bitcast(FP8X4),
+                        scales=ws[n][:, P * b0:P * (b0 + nb)],
+                        in_=g[:, 4 * P * b0:4 * P * (b0 + nb)],
+                    )
+
+        def cell(acc_ap, t, i):
+            ng = neighbours(i)
+            for gi, g in enumerate(ng):
+                nc.tensor.matmul_mx(
+                    out=acc_ap,
+                    lhsT=xc[t][:, P * g:P * (g + 1)].bitcast(FP8X4),
+                    lhsT_scale=xs[t][:, P * g:P * (g + 1)],
+                    rhs=wc[i][:, P * gi:P * (gi + 1)].bitcast(FP8X4),
+                    rhs_scale=ws[i][:, P * gi:P * (gi + 1)],
+                    start=(gi == 0),
+                    stop=(gi == len(ng) - 1),
+                )
+
+        def stage_multiply(step):
+            kind, n = step
+            if kind == "w":
+                acc = psum_a.tile([P, 4, O], F32, name="acc", tag="acc")
+                for t in range(NF):
+                    cell(acc[:, t, :], t, n)
+                accs[step] = [acc]
+            elif n >= NF:
+                accs[step] = []
+                for h in range(2):
+                    acc = psum_a.tile([P, 4, O], F32, name="acc", tag="acc")
+                    for c in range(4):
+                        cell(acc[:, c, :], n, 4 * h + c)
+                    accs[step] = accs[step] + [acc]
+
+        osb_first = keep.tile([P, NF, J * O], F32, name="osb_first")
+
+        def stage_output(step):
+            kind, n = step
+            if kind == "w":
+                nc.vector.tensor_tensor(
+                    out=osb_first[:, :, O * n:O * (n + 1)],
+                    in0=accs[step][0][:],
+                    in1=bias_bc[:, O * n:O * (n + 1)].unsqueeze(1).to_broadcast([P, NF, O]),
+                    op=ADD,
+                )
+                if n == J - 1:
+                    nc.sync.dma_start(out=out_view[:, 0:NF, :], in_=osb_first[:])
+            elif n >= NF:
+                osb = keep.tile([P, J * O], F32, name="osb%d" % n)
+                for h in range(2):
+                    nc.vector.tensor_tensor(
+                        out=osb[:, 512 * h:512 * (h + 1)],
+                        in0=accs[step][h][:].rearrange("p c o -> p (c o)"),
+                        in1=bias_bc[:, 512 * h:512 * (h + 1)],
+                        op=ADD,
+                    )
+                    if n >= 6:
+                        nc.sync.dma_start(out=out_view[:, n, 512 * h:512 * (h + 1)], in_=osb[:, 512 * h:512 * (h + 1)])
+                if n < 6:
+                    nc.sync.dma_start(out=out_view[:, n, :], in_=osb[:])
+
+        for t in range(NF):
+            load_x(t)
+            if t == 0:
+                nc.sync.dma_start(out=brow[0:1, :], in_=bias.rearrange("(a n) -> a n", a=1))
+        for i in range(J):
+            load_w(i)
+
+        for n in range(N + 2):
+            if n < N:
+                stage_mask(steps[n])
+                stage_transpose(steps[n])
+                if n < NT - NF:
+                    load_x(NF + n)
+                if n == 1:
+                    bias_spread()
+            if 1 <= n <= N:
+                stage_quantise(steps[n - 1])
+                stage_multiply(steps[n - 1])
+            if n >= 2:
+                stage_output(steps[n - 2])

@@ -18,7 +18,10 @@ NBLK = 3 * J - 2
 FLOPS = 2 * B * O * I * NBLK
 BYTES = 2 * B * J * I + 2 * 2 * NBLK * O * I + 2 * J * O + 4 * B * J * O
 
-NF = 4
+STEPS = [("x", 0, 0, 8), ("x", 1, 0, 8), ("x", 2, 0, 8), ("w", 0), ("x", 3, 0, 8), ("w", 1), ("w", 2), ("w", 3), ("w", 4), ("w", 5), ("w", 6), ("w", 7), ("x", 4, 0, 8), ("x", 5, 0, 8), ("x", 6, 0, 8), ("x", 7, 0, 8)]
+GROUPS = [1, 1, 1, 1, 1, 1, 1, 1, 1, 1, 1, 1, 1, 1, 1, 1]
+PERM = (12,13,14,15,)
+AHEAD = 1
 
 
 def neighbours(i):
@@ -31,9 +34,10 @@ def tile_skeletonlinear_kernel(tc, x, weight, mask, bias, out):
         const = ctx.enter_context(tc.tile_pool(name="const", bufs=1))
         keep = ctx.enter_context(tc.tile_pool(name="keep", bufs=1))
         xraw = ctx.enter_context(tc.tile_pool(name="xraw", bufs=4))
+        wraw = ctx.enter_context(tc.tile_pool(name="wraw", bufs=8))
         grp = ctx.enter_context(tc.tile_pool(name="grp", bufs=3))
         psum_t = ctx.enter_context(tc.psum_pool(name="psum_t", bufs=4))
-        psum_a = ctx.enter_context(tc.psum_pool(name="psum_a", bufs=4))
+        psum_a = ctx.enter_context(tc.psum_pool(name="psum_a", bufs=8 - 4))
         ctx.enter_context(tc.manual_schedule())
 
         x_view = x.rearrange("(t p) k -> p t k", p=P)
@@ -47,28 +51,45 @@ def tile_skeletonlinear_kernel(tc, x, weight, mask, bias, out):
         nc.vector.memset(brow[:], 0.0)
         bias_bc = const.tile([P, J * O], F32, name="bias_bc")
 
-        xr = {}
-        wr = {}
-        mr = {}
+        raw = {}
+        msk = {}
+        words = {}
         gt = {}
-        xc = {}
-        xs = {}
-        wc = {}
-        ws = {}
         accs = {}
+        xc = []
+        xs = []
+        wc = []
+        ws = []
+        for t in range(NT):
+            cx = keep.tile([P, J * P], U32, name="xc%d" % t, align_bytes=64)
+            sx = keep.tile([P, J * P], U8, name="xs%d" % t, align_bytes=64)
+            xc.append(cx)
+            xs.append(sx)
+        for i in range(J):
+            cw = keep.tile([P, len(neighbours(i)) * P], U32, name="wc%d" % i, align_bytes=64)
+            sw = keep.tile([P, len(neighbours(i)) * P], U8, name="ws%d" % i, align_bytes=64)
+            wc.append(cw)
+            ws.append(sw)
+        osb = keep.tile([P, NT, J * O], F32, name="osb")
 
-        def load_x(t):
-            xr[t] = xraw.tile([P, J * I], BF16, name="xr%d" % t, tag="xr")
-            nc.sync.dma_start(out=xr[t][:], in_=x_view[:, t, :])
+        N = len(STEPS)
+        def blocks(n):
+            s = STEPS[n]
+            return len(neighbours(s[1])) if s[0] == "w" else s[3] - s[2]
 
-        def load_w(i):
-            ng = neighbours(i)
-            n = len(ng) * I
-            lo = ng[0] * I
-            wr[i] = keep.tile([P, n], BF16, name="wr%d" % i)
-            mr[i] = keep.tile([P, n], BF16, name="mr%d" % i)
-            nc.sync.dma_start(out=wr[i][:], in_=weight[i * O:(i + 1) * O, lo:lo + n])
-            nc.sync.dma_start(out=mr[i][:], in_=mask[i * O:(i + 1) * O, lo:lo + n])
+        def load(n):
+            s = STEPS[n]
+            w = blocks(n) * I
+            if s[0] == "x":
+                raw[n] = xraw.tile([P, w], BF16, name="xr%d" % n, tag="xr")
+                nc.sync.dma_start(out=raw[n][:], in_=x_view[:, s[1], s[2] * I:s[3] * I])
+            else:
+                i = s[1]
+                lo = neighbours(i)[0] * I
+                raw[n] = wraw.tile([P, w], BF16, name="wr%d" % n, tag="wr")
+                msk[n] = wraw.tile([P, w], BF16, name="mr%d" % n, tag="mr")
+                nc.sync.dma_start(out=raw[n][:], in_=weight[i * O:(i + 1) * O, lo:lo + w])
+                nc.sync.dma_start(out=msk[n][:], in_=mask[i * O:(i + 1) * O, lo:lo + w])
 
         def bias_spread():
             for h in range(2):
@@ -76,63 +97,56 @@ def tile_skeletonlinear_kernel(tc, x, weight, mask, bias, out):
                 nc.tensor.matmul(out=pb[:], lhsT=ones[:], rhs=brow[:, 512 * h:512 * (h + 1)], start=True, stop=True)
                 nc.vector.tensor_copy(out=bias_bc[:, 512 * h:512 * (h + 1)], in_=pb[:])
 
-        def transpose_group(src32, nblk, g32, dve_banks):
-            for b0 in range(0, nblk, 2):
-                nb = min(2, nblk - b0)
+        def stage_words(n):
+            s = STEPS[n]
+            nb = blocks(n)
+            if s[0] == "w":
+                wp = wraw.tile([P, nb * I], BF16, name="wp%d" % n, tag="wp", bufs=3)
+                nc.vector.tensor_tensor(
+                    out=wp[:].rearrange("p (u m e) -> p u m e", u=2, e=2),
+                    in0=raw[n][:].rearrange("p (m u e) -> p u m e", u=2, e=2),
+                    in1=msk[n][:].rearrange("p (m u e) -> p u m e", u=2, e=2),
+                    op=MULT)
+                words[n] = wp[:].bitcast(F32).rearrange("p (u m) -> p u m", u=2)
+            elif n in PERM:
+                xp = xraw.tile([P, nb * I // 2], F32, name="xp%d" % n, tag="xp", bufs=2)
+                nc.vector.tensor_copy(
+                    out=xp[:].rearrange("p (u m) -> p u m", u=2),
+                    in_=raw[n][:].bitcast(F32).rearrange("p (m u) -> p u m", u=2))
+                words[n] = xp[:].rearrange("p (u m) -> p u m", u=2)
+            else:
+                words[n] = raw[n][:].bitcast(F32).rearrange("p (m u) -> p u m", u=2)
+
+        def stage_transpose(n):
+            nb = blocks(n)
+            big = STEPS[n][0] == "x"
+            g = grp.tile([P, 4 * nb * P], BF16, name="g%d" % n, tag="gx" if big else "gw", align_bytes=64)
+            g32 = g[:].bitcast(F32).rearrange("p (g r u) -> p g r u", g=nb, r=P, u=2)
+            for b0 in range(0, nb, 2):
+                k = min(2, nb - b0)
                 tp = psum_t.tile([P, 2, 2, P], F32, name="tp", tag="tp")
-                for gg in range(nb):
+                for gg in range(k):
                     for u in range(2):
-                        c0 = 256 * (b0 + gg)
-                        nc.tensor.transpose(out=tp[:, gg, u, :], in_=src32[:, c0 + u:c0 + 256:2], identity=ident[:])
-                src = tp[:, 0:nb, :, :].rearrange("p g u r -> p g r u")
-                if b0 // 2 in dve_banks:
-                    nc.vector.tensor_copy(out=g32[:, b0:b0 + nb, :, :], in_=src)
-                else:
-                    nc.scalar.copy(out=g32[:, b0:b0 + nb, :, :], in_=src)
+                        nc.tensor.transpose(out=tp[:, gg, u, :], in_=words[n][:, u, P * (b0 + gg):P * (b0 + gg + 1)], identity=ident[:])
+                nc.scalar.copy(out=g32[:, b0:b0 + k, :, :], in_=tp[:, 0:k, :, :].rearrange("p g u r -> p g r u"))
+            gt[n] = g
 
-        steps = [("x", t) for t in range(NF)] + [("w", i) for i in range(J)] + [("x", t) for t in range(NF, NT)]
-        N = len(steps)
-
-        def stage_mask(step):
-            kind, i = step
-            if kind == "w":
-                nc.vector.tensor_tensor(out=wr[i][:], in0=wr[i][:], in1=mr[i][:], op=MULT)
-
-        def stage_transpose(step):
-            kind, n = step
-            if kind == "x":
-                g = grp.tile([P, 4 * J * P], BF16, name="gx", tag="gx", align_bytes=64)
-                g32 = g[:].bitcast(F32).rearrange("p (g r u) -> p g r u", g=J, r=P, u=2)
-                transpose_group(xr[n][:].bitcast(F32), J, g32, [])
+        def stage_quantise(n):
+            s = STEPS[n]
+            nb = blocks(n)
+            if s[0] == "x":
+                codes, scales, c0 = xc[s[1]], xs[s[1]], s[2]
             else:
-                g = grp.tile([P, 4 * 3 * P], BF16, name="gw", tag="gw", align_bytes=64)
-                g32 = g[:].bitcast(F32).rearrange("p (g r u) -> p g r u", g=3, r=P, u=2)
-                transpose_group(wr[n][:].bitcast(F32), len(neighbours(n)), g32, [])
-            gt[step] = g
-
-        def stage_quantise(step):
-            kind, n = step
-            g = gt[step]
-            if kind == "x":
-                xc[n] = keep.tile([P, J * P], U32, name="xc%d" % n, align_bytes=64)
-                xs[n] = keep.tile([P, J * P], U8, name="xs%d" % n, align_bytes=64)
-                for h in range(2):
-                    nc.vector.quantize_mx(
-                        out=xc[n][:, 512 * h:512 * (h + 1)].bitcast(FP8X4),
-                        scales=xs[n][:, 512 * h:512 * (h + 1)],
-                        in_=g[:, 2048 * h:2048 * (h + 1)],
-                    )
-            else:
-                nblk = len(neighbours(n))
-                wc[n] = keep.tile([P, 3 * P], U32, name="wc%d" % n, align_bytes=64)
-                ws[n] = keep.tile([P, 3 * P], U8, name="ws%d" % n, align_bytes=64)
-                for b0 in range(0, nblk, 2):
-                    nb = min(2, nblk - b0)
-                    nc.vector.quantize_mx(
-                        out=wc[n][:, P * b0:P * (b0 + nb)].bitcast(FP8X4),
-                        scales=ws[n][:, P * b0:P * (b0 + nb)],
-                        in_=g[:, 4 * P * b0:4 * P * (b0 + nb)],
-                    )
+                codes, scales, c0 = wc[s[1]], ws[s[1]], 0
+            b0 = 0
+            while b0 < nb:
+                k = 4 if nb - b0 >= 4 else 2 if nb - b0 >= 2 else 1
+                lo, hi = P * (c0 + b0), P * (c0 + b0 + k)
+                nc.vector.quantize_mx(
+                    out=codes[:, lo:hi].bitcast(FP8X4),
+                    scales=scales[:, lo:hi],
+                    in_=gt[n][:, 4 * P * b0:4 * P * (b0 + k)])
+                b0 = b0 + k
 
         def cell(acc_ap, t, i):
             ng = neighbours(i)
@@ -147,65 +161,120 @@ def tile_skeletonlinear_kernel(tc, x, weight, mask, bias, out):
                     stop=(gi == len(ng) - 1),
                 )
 
-        def stage_multiply(step):
-            kind, n = step
-            if kind == "w":
-                acc = psum_a.tile([P, 4, O], F32, name="acc", tag="acc")
-                for t in range(NF):
-                    cell(acc[:, t, :], t, n)
-                accs[step] = [acc]
-            elif n >= NF:
-                accs[step] = []
-                for h in range(2):
+        have_x = set()
+        have_w = set()
+        made = set()
+        stored = set()
+
+        def stage_multiply(n):
+            s = STEPS[n]
+            accs[n] = []
+            if s[0] == "w":
+                have_w.add(s[1])
+                i = s[1]
+                ts = [t for t in range(NT) if (t, i) not in made and all((t, g) in have_x for g in neighbours(i))]
+                runs = [ts[a:a + 4] for a in range(0, len(ts), 4)]
+                for r in runs:
                     acc = psum_a.tile([P, 4, O], F32, name="acc", tag="acc")
-                    for c in range(4):
-                        cell(acc[:, c, :], n, 4 * h + c)
-                    accs[step] = accs[step] + [acc]
+                    for c, t in enumerate(r):
+                        cell(acc[:, c, :], t, i)
+                        made.add((t, i))
+                    accs[n].append((acc, r, [i]))
+            else:
+                t = s[1]
+                for g in range(s[2], s[3]):
+                    have_x.add((t, g))
+                js = [i for i in range(J) if i in have_w and (t, i) not in made and all((t, g) in have_x for g in neighbours(i))]
+                runs = [js[a:a + 4] for a in range(0, len(js), 4)]
+                for r in runs:
+                    acc = psum_a.tile([P, 4, O], F32, name="acc", tag="acc")
+                    for c, i in enumerate(r):
+                        cell(acc[:, c, :], t, i)
+                        made.add((t, i))
+                    accs[n].append((acc, [t], r))
 
-        osb_first = keep.tile([P, NF, J * O], F32, name="osb_first")
+        added = set()
 
-        def stage_output(step):
-            kind, n = step
-            if kind == "w":
-                nc.vector.tensor_tensor(
-                    out=osb_first[:, :, O * n:O * (n + 1)],
-                    in0=accs[step][0][:],
-                    in1=bias_bc[:, O * n:O * (n + 1)].unsqueeze(1).to_broadcast([P, NF, O]),
-                    op=ADD,
-                )
-                if n == J - 1:
-                    nc.sync.dma_start(out=out_view[:, 0:NF, :], in_=osb_first[:])
-            elif n >= NF:
-                osb = keep.tile([P, J * O], F32, name="osb%d" % n)
-                for h in range(2):
+        def stage_output(n):
+            for acc, ts, js in accs[n]:
+                cols = slice(O * js[0], O * (js[-1] + 1))
+                if len(js) == 1:
+                    k = len(ts)
                     nc.vector.tensor_tensor(
-                        out=osb[:, 512 * h:512 * (h + 1)],
-                        in0=accs[step][h][:].rearrange("p c o -> p (c o)"),
-                        in1=bias_bc[:, 512 * h:512 * (h + 1)],
-                        op=ADD,
-                    )
-                    if n >= 6:
-                        nc.sync.dma_start(out=out_view[:, n, 512 * h:512 * (h + 1)], in_=osb[:, 512 * h:512 * (h + 1)])
-                if n < 6:
-                    nc.sync.dma_start(out=out_view[:, n, :], in_=osb[:])
+                        out=osb[:, ts[0]:ts[0] + k, cols],
+                        in0=acc[:, 0:k, :],
+                        in1=bias_bc[:, cols].unsqueeze(1).to_broadcast([P, k, O]),
+                        op=ADD)
+                else:
+                    nc.vector.tensor_tensor(
+                        out=osb[:, ts[0], cols],
+                        in0=acc[:, 0:len(js), :].rearrange("p c o -> p (c o)"),
+                        in1=bias_bc[:, cols],
+                        op=ADD)
+                for t in ts:
+                    for i in js:
+                        added.add((t, i))
+                if n >= N - 2:
+                    nc.sync.dma_start(out=out_view[:, ts[0], cols], in_=osb[:, ts[0], cols])
+                    for i in js:
+                        stored.add((ts[0], i))
+            q = 4
+            full = [t for t in range(NT) if all((t, i) in added and (t, i) not in stored for i in range(J))]
+            if len(full) == 1:
+                t = full[0]
+                nc.sync.dma_start(out=out_view[:, t, :], in_=osb[:, t, :])
+                for i in range(J):
+                    stored.add((t, i))
+            for h in range(J // q):
+                ts = [t for t in range(NT) if all((t, i) in added and (t, i) not in stored for i in range(q * h, q * h + q))]
+                while ts:
+                    r = [t for t in ts if t - ts[0] < 4 and all(z in ts for z in range(ts[0], t + 1))]
+                    cols = slice(O * q * h, O * q * (h + 1))
+                    nc.sync.dma_start(out=out_view[:, r[0]:r[-1] + 1, cols], in_=osb[:, r[0]:r[-1] + 1, cols])
+                    for t in r:
+                        for i in range(q * h, q * h + q):
+                            stored.add((t, i))
+                    ts = [t for t in ts if t not in r]
 
-        for t in range(NF):
-            load_x(t)
-            if t == 0:
-                nc.sync.dma_start(out=brow[0:1, :], in_=bias.rearrange("(a n) -> a n", a=1))
-        for i in range(J):
-            load_w(i)
+        loaded = []
 
-        for n in range(N + 2):
-            if n < N:
-                stage_mask(steps[n])
-                stage_transpose(steps[n])
-                if n < NT - NF:
-                    load_x(NF + n)
-                if n == 1:
+        def load_ahead(n):
+            while len(loaded) < N:
+                k = len(loaded)
+                kind = STEPS[k][0]
+                busy = [z for z in loaded if STEPS[z][0] == kind and z >= n]
+                if len(busy) >= (4 if kind == "x" else 8):
+                    break
+                load(k)
+                loaded.append(k)
+                if k == 0:
+                    nc.sync.dma_start(out=brow[0:1, :], in_=bias.rearrange("(a n) -> a n", a=1))
+
+        load_ahead(0)
+        groups = []
+        for size in GROUPS:
+            lo = groups[-1][-1] + 1 if groups else 0
+            groups.append(list(range(lo, lo + size)))
+        NG = len(groups)
+        for n in range(AHEAD):
+            for k in groups[n]:
+                stage_words(k)
+        for n in range(NG + 2):
+            if n < NG:
+                for k in groups[n]:
+                    stage_transpose(k)
+                    load_ahead(k + 1)
+                if n == 0:
                     bias_spread()
-            if 1 <= n <= N:
-                stage_quantise(steps[n - 1])
-                stage_multiply(steps[n - 1])
+            if 1 <= n <= NG:
+                for k in groups[n - 1]:
+                    stage_quantise(k)
+            if n + AHEAD < NG:
+                for k in groups[n + AHEAD]:
+                    stage_words(k)
+            if 1 <= n <= NG:
+                for k in groups[n - 1]:
+                    stage_multiply(k)
             if n >= 2:
-                stage_output(steps[n - 2])
+                for k in groups[n - 2]:
+                    stage_output(k)

@@ -19,9 +19,10 @@ FLOPS = 2 * B * O * I * NBLK
 BYTES = 2 * B * J * I + 2 * 2 * NBLK * O * I + 2 * J * O + 4 * B * J * O
 
 STEPS = [("x", 0, 0, 8), ("x", 1, 0, 8), ("x", 2, 0, 8), ("w", 0), ("x", 3, 0, 8), ("w", 1), ("w", 2), ("w", 3), ("w", 4), ("w", 5), ("w", 6), ("w", 7), ("x", 4, 0, 8), ("x", 5, 0, 8), ("x", 6, 0, 8), ("x", 7, 0, 8)]
-GROUPS = [1, 1, 1, 1, 1, 1, 1, 1, 1, 1, 1, 1, 1, 1, 1, 1]
-PERM = (12,13,14,15,)
-AHEAD = 1
+PERM = {12: (2, 1), 13: (2, 1), 14: (2, 1), 15: (2, 1)}
+AHEAD = 2
+LAG = 2
+HALF = 4
 
 
 def neighbours(i):
@@ -55,7 +56,6 @@ def tile_skeletonlinear_kernel(tc, x, weight, mask, bias, out):
         msk = {}
         words = {}
         gt = {}
-        accs = {}
         xc = []
         xs = []
         wc = []
@@ -73,6 +73,18 @@ def tile_skeletonlinear_kernel(tc, x, weight, mask, bias, out):
         osb = keep.tile([P, NT, J * O], F32, name="osb")
 
         N = len(STEPS)
+        runs = []
+        last = {}
+        for n in range(N):
+            s = STEPS[n]
+            if s[0] == "x":
+                for b0 in range(0, s[3] - s[2], HALF):
+                    runs.append((n, b0, min(HALF, s[3] - s[2] - b0)))
+            else:
+                runs.append((n, 0, len(neighbours(s[1]))))
+            last[n] = len(runs) - 1
+        R = len(runs)
+
         def blocks(n):
             s = STEPS[n]
             return len(neighbours(s[1])) if s[0] == "w" else s[3] - s[2]
@@ -95,58 +107,68 @@ def tile_skeletonlinear_kernel(tc, x, weight, mask, bias, out):
             for h in range(2):
                 pb = psum_a.tile([P, 512], F32, name="pb", tag="acc")
                 nc.tensor.matmul(out=pb[:], lhsT=ones[:], rhs=brow[:, 512 * h:512 * (h + 1)], start=True, stop=True)
-                nc.vector.tensor_copy(out=bias_bc[:, 512 * h:512 * (h + 1)], in_=pb[:])
+                nc.scalar.copy(out=bias_bc[:, 512 * h:512 * (h + 1)], in_=pb[:])
 
-        def stage_words(n):
+        def stage_words(r):
+            n, b0, nb = runs[r]
             s = STEPS[n]
-            nb = blocks(n)
             if s[0] == "w":
-                wp = wraw.tile([P, nb * I], BF16, name="wp%d" % n, tag="wp", bufs=3)
+                wp = wraw.tile([P, nb * I], BF16, name="wp%d" % r, tag="wp", bufs=3)
                 nc.vector.tensor_tensor(
                     out=wp[:].rearrange("p (u m e) -> p u m e", u=2, e=2),
                     in0=raw[n][:].rearrange("p (m u e) -> p u m e", u=2, e=2),
                     in1=msk[n][:].rearrange("p (m u e) -> p u m e", u=2, e=2),
                     op=MULT)
-                words[n] = wp[:].bitcast(F32).rearrange("p (u m) -> p u m", u=2)
-            elif n in PERM:
-                xp = xraw.tile([P, nb * I // 2], F32, name="xp%d" % n, tag="xp", bufs=2)
-                nc.vector.tensor_copy(
-                    out=xp[:].rearrange("p (u m) -> p u m", u=2),
-                    in_=raw[n][:].bitcast(F32).rearrange("p (m u) -> p u m", u=2))
-                words[n] = xp[:].rearrange("p (u m) -> p u m", u=2)
-            else:
-                words[n] = raw[n][:].bitcast(F32).rearrange("p (m u) -> p u m", u=2)
+                words[r] = [(0, nb, wp[:].bitcast(F32).rearrange("p (u m) -> p u m", u=2))]
+                return
+            src = raw[n][:].bitcast(F32)[:, 256 * b0:256 * (b0 + nb)]
+            dve, act = PERM.get(n, (0, 0))
+            c1 = nb - act
+            c0 = c1 - dve
+            words[r] = [(0, c0, src.rearrange("p (m u) -> p u m", u=2))]
+            if dve + act > 0:
+                xp = xraw.tile([P, nb * I // 2], F32, name="xp%d" % r, tag="xp", bufs=3)
+                for put, lo, hi in ((nc.vector.tensor_copy, c0, c1), (nc.scalar.copy, c1, nb)):
+                    if hi > lo:
+                        dst = xp[:, 256 * lo:256 * hi].rearrange("p (u m) -> p u m", u=2)
+                        put(out=dst, in_=src[:, 256 * lo:256 * hi].rearrange("p (m u) -> p u m", u=2))
+                        words[r].append((lo, hi, dst))
 
-        def stage_transpose(n):
-            nb = blocks(n)
-            big = STEPS[n][0] == "x"
-            g = grp.tile([P, 4 * nb * P], BF16, name="g%d" % n, tag="gx" if big else "gw", align_bytes=64)
-            g32 = g[:].bitcast(F32).rearrange("p (g r u) -> p g r u", g=nb, r=P, u=2)
+        def word_block(r, b, u):
+            for lo, hi, view in words[r]:
+                if lo <= b < hi:
+                    return view[:, u, P * (b - lo):P * (b - lo + 1)]
+
+        def stage_transpose(r):
+            n, first, nb = runs[r]
+            g = grp.tile([P, 4 * nb * P], BF16, name="g%d" % r, tag="gx" if STEPS[n][0] == "x" else "gw", align_bytes=64)
+            g32 = g[:].bitcast(F32).rearrange("p (g r u) -> p g r u", r=P, u=2)
             for b0 in range(0, nb, 2):
                 k = min(2, nb - b0)
                 tp = psum_t.tile([P, 2, 2, P], F32, name="tp", tag="tp")
                 for gg in range(k):
                     for u in range(2):
-                        nc.tensor.transpose(out=tp[:, gg, u, :], in_=words[n][:, u, P * (b0 + gg):P * (b0 + gg + 1)], identity=ident[:])
-                nc.scalar.copy(out=g32[:, b0:b0 + k, :, :], in_=tp[:, 0:k, :, :].rearrange("p g u r -> p g r u"))
-            gt[n] = g
+                        nc.tensor.transpose(out=tp[:, gg, u, :], in_=word_block(r, b0 + gg, u), identity=ident[:])
+                put = nc.vector.tensor_copy if (r, b0) in () else nc.scalar.copy
+                put(out=g32[:, b0:b0 + k, :, :], in_=tp[:, 0:k, :, :].rearrange("p g u r -> p g r u"))
+            gt[r] = g
 
-        def stage_quantise(n):
+        def stage_quantise(r):
+            n, first, nb = runs[r]
             s = STEPS[n]
-            nb = blocks(n)
             if s[0] == "x":
-                codes, scales, c0 = xc[s[1]], xs[s[1]], s[2]
+                codes, scales, c0 = xc[s[1]], xs[s[1]], s[2] + first
             else:
                 codes, scales, c0 = wc[s[1]], ws[s[1]], 0
             b0 = 0
-            while b0 < nb:
-                k = 4 if nb - b0 >= 4 else 2 if nb - b0 >= 2 else 1
-                lo, hi = P * (c0 + b0), P * (c0 + b0 + k)
-                nc.vector.quantize_mx(
-                    out=codes[:, lo:hi].bitcast(FP8X4),
-                    scales=scales[:, lo:hi],
-                    in_=gt[n][:, 4 * P * b0:4 * P * (b0 + k)])
-                b0 = b0 + k
+            for k in (4, 2, 1):
+                while nb - b0 >= k:
+                    lo, hi = P * (c0 + b0), P * (c0 + b0 + k)
+                    nc.vector.quantize_mx(
+                        out=codes[:, lo:hi].bitcast(FP8X4),
+                        scales=scales[:, lo:hi],
+                        in_=gt[r][:, 4 * P * b0:4 * P * (b0 + k)])
+                    b0 = b0 + k
 
         def cell(acc_ap, t, i):
             ng = neighbours(i)
@@ -164,85 +186,91 @@ def tile_skeletonlinear_kernel(tc, x, weight, mask, bias, out):
         have_x = set()
         have_w = set()
         made = set()
+        added = set()
         stored = set()
+        queue = []
+        accs = {}
 
-        def stage_multiply(n):
+        def ready(t, i):
+            return i in have_w and (t, i) not in made and all((t, g) in have_x for g in neighbours(i))
+
+        def open_cells(r):
+            n, first, nb = runs[r]
             s = STEPS[n]
-            accs[n] = []
             if s[0] == "w":
                 have_w.add(s[1])
-                i = s[1]
-                ts = [t for t in range(NT) if (t, i) not in made and all((t, g) in have_x for g in neighbours(i))]
-                runs = [ts[a:a + 4] for a in range(0, len(ts), 4)]
-                for r in runs:
-                    acc = psum_a.tile([P, 4, O], F32, name="acc", tag="acc")
-                    for c, t in enumerate(r):
-                        cell(acc[:, c, :], t, i)
-                        made.add((t, i))
-                    accs[n].append((acc, r, [i]))
+                cells = [(t, s[1]) for t in range(NT) if ready(t, s[1])]
             else:
-                t = s[1]
-                for g in range(s[2], s[3]):
-                    have_x.add((t, g))
-                js = [i for i in range(J) if i in have_w and (t, i) not in made and all((t, g) in have_x for g in neighbours(i))]
-                runs = [js[a:a + 4] for a in range(0, len(js), 4)]
-                for r in runs:
-                    acc = psum_a.tile([P, 4, O], F32, name="acc", tag="acc")
-                    for c, i in enumerate(r):
-                        cell(acc[:, c, :], t, i)
-                        made.add((t, i))
-                    accs[n].append((acc, [t], r))
+                for g in range(first, first + nb):
+                    have_x.add((s[1], s[2] + g))
+                cells = [(s[1], i) for i in range(J) if ready(s[1], i)]
+                if r != last[n]:
+                    cells = []
+            for z in cells:
+                made.add(z)
+            for a in range(0, len(cells), 4):
+                queue.append((r + LAG, n, cells[a:a + 4]))
 
-        added = set()
+        def stage_multiply(r):
+            accs[r] = []
+            count = 0
+            while queue and queue[0][0] <= r and (count < 1 or STEPS[queue[0][1]][0] == "w" or r >= R):
+                due, n, cells = queue.pop(0)
+                acc = psum_a.tile([P, 4, O], F32, name="acc", tag="acc")
+                for c, (t, i) in enumerate(cells):
+                    cell(acc[:, c, :], t, i)
+                accs[r].append((acc, n, cells))
+                count = count + 1
 
-        def stage_output(n):
-            for acc, ts, js in accs[n]:
-                cols = slice(O * js[0], O * (js[-1] + 1))
-                if len(js) == 1:
-                    k = len(ts)
+        def stage_output(r):
+            for acc, n, cells in accs[r]:
+                t, i = cells[0]
+                k = len(cells)
+                if STEPS[n][0] == "w":
+                    cols = slice(O * i, O * (i + 1))
                     nc.vector.tensor_tensor(
-                        out=osb[:, ts[0]:ts[0] + k, cols],
+                        out=osb[:, t:t + k, cols],
                         in0=acc[:, 0:k, :],
                         in1=bias_bc[:, cols].unsqueeze(1).to_broadcast([P, k, O]),
                         op=ADD)
                 else:
+                    cols = slice(O * i, O * (i + k))
                     nc.vector.tensor_tensor(
-                        out=osb[:, ts[0], cols],
-                        in0=acc[:, 0:len(js), :].rearrange("p c o -> p (c o)"),
+                        out=osb[:, t, cols],
+                        in0=acc[:, 0:k, :].rearrange("p c o -> p (c o)"),
                         in1=bias_bc[:, cols],
                         op=ADD)
-                for t in ts:
-                    for i in js:
-                        added.add((t, i))
+                for z in cells:
+                    added.add(z)
                 if n >= N - 2:
-                    nc.sync.dma_start(out=out_view[:, ts[0], cols], in_=osb[:, ts[0], cols])
-                    for i in js:
-                        stored.add((ts[0], i))
-            q = 4
-            full = [t for t in range(NT) if all((t, i) in added and (t, i) not in stored for i in range(J))]
-            if len(full) == 1:
-                t = full[0]
-                nc.sync.dma_start(out=out_view[:, t, :], in_=osb[:, t, :])
-                for i in range(J):
-                    stored.add((t, i))
-            for h in range(J // q):
-                ts = [t for t in range(NT) if all((t, i) in added and (t, i) not in stored for i in range(q * h, q * h + q))]
-                while ts:
-                    r = [t for t in ts if t - ts[0] < 4 and all(z in ts for z in range(ts[0], t + 1))]
-                    cols = slice(O * q * h, O * q * (h + 1))
-                    nc.sync.dma_start(out=out_view[:, r[0]:r[-1] + 1, cols], in_=osb[:, r[0]:r[-1] + 1, cols])
-                    for t in r:
-                        for i in range(q * h, q * h + q):
+                    nc.sync.dma_start(out=out_view[:, t, cols], in_=osb[:, t, cols])
+                    for z in cells:
+                        stored.add(z)
+            for h in range(2):
+                mine = range(4 * h, 4 * h + 4)
+                ts = [t for t in range(NT) if all((t, i) in added and (t, i) not in stored for i in mine)]
+                if len(ts) == 1 and h == 0 and ts[0] >= 4:
+                    continue
+                if len(ts) == 1 and h == 1 and (ts[0], 0) not in stored:
+                    t = ts[0]
+                    nc.sync.dma_start(out=out_view[:, t, :], in_=osb[:, t, :])
+                    for i in range(J):
+                        stored.add((t, i))
+                    continue
+                if ts:
+                    cols = slice(512 * h, 512 * (h + 1))
+                    nc.sync.dma_start(out=out_view[:, ts[0]:ts[-1] + 1, cols], in_=osb[:, ts[0]:ts[-1] + 1, cols])
+                    for t in ts:
+                        for i in mine:
                             stored.add((t, i))
-                    ts = [t for t in ts if t not in r]
 
         loaded = []
 
-        def load_ahead(n):
+        def load_ahead(r):
             while len(loaded) < N:
                 k = len(loaded)
                 kind = STEPS[k][0]
-                busy = [z for z in loaded if STEPS[z][0] == kind and z >= n]
+                busy = [z for z in loaded if STEPS[z][0] == kind and last[z] >= r]
                 if len(busy) >= (4 if kind == "x" else 8):
                     break
                 load(k)
@@ -251,30 +279,19 @@ def tile_skeletonlinear_kernel(tc, x, weight, mask, bias, out):
                     nc.sync.dma_start(out=brow[0:1, :], in_=bias.rearrange("(a n) -> a n", a=1))
 
         load_ahead(0)
-        groups = []
-        for size in GROUPS:
-            lo = groups[-1][-1] + 1 if groups else 0
-            groups.append(list(range(lo, lo + size)))
-        NG = len(groups)
-        for n in range(AHEAD):
-            for k in groups[n]:
-                stage_words(k)
-        for n in range(NG + 2):
-            if n < NG:
-                for k in groups[n]:
-                    stage_transpose(k)
-                    load_ahead(k + 1)
-                if n == 0:
+        for r in range(AHEAD):
+            stage_words(r)
+        for r in range(R + LAG + 3):
+            if 1 <= r <= R:
+                stage_quantise(r - 1)
+                open_cells(r - 1)
+            if r < R:
+                stage_transpose(r)
+                load_ahead(r + 1)
+                if r == 1:
                     bias_spread()
-            if 1 <= n <= NG:
-                for k in groups[n - 1]:
-                    stage_quantise(k)
-            if n + AHEAD < NG:
-                for k in groups[n + AHEAD]:
-                    stage_words(k)
-            if 1 <= n <= NG:
-                for k in groups[n - 1]:
-                    stage_multiply(k)
-            if n >= 2:
-                for k in groups[n - 2]:
-                    stage_output(k)
+            stage_multiply(r)
+            if r + AHEAD < R:
+                stage_words(r + AHEAD)
+            if r >= 1:
+                stage_output(r - 1)

@@ -18,7 +18,7 @@ NBLK = 3 * J - 2
 FLOPS = 2 * B * O * I * NBLK
 BYTES = 2 * B * J * I + 2 * 2 * NBLK * O * I + 2 * J * O + 4 * B * J * O
 
-STEPS = [("x", 0, 0, 8), ("x", 1, 0, 8), ("x", 2, 0, 8), ("w", 0), ("x", 3, 0, 8), ("w", 1), ("w", 2), ("w", 3), ("w", 4), ("w", 5), ("w", 6), ("w", 7), ("x", 4, 0, 8), ("x", 5, 0, 8), ("x", 6, 0, 8), ("x", 7, 0, 8)]
+STEPS = [("x", 0, 0, 8), ("w", 0), ("x", 1, 0, 8), ("w", 1), ("x", 2, 0, 8), ("w", 2), ("x", 3, 0, 8), ("w", 3), ("w", 4), ("w", 5), ("w", 6), ("w", 7), ("x", 4, 0, 8), ("x", 5, 0, 8), ("x", 6, 0, 8), ("x", 7, 0, 8)]
 PERM = {12: (2, 1), 13: (2, 1), 14: (2, 1), 15: (2, 1)}
 AHEAD = 2
 LAG = 2

@@ -19,7 +19,7 @@ FLOPS = 2 * B * O * I * NBLK
 BYTES = 2 * B * J * I + 2 * 2 * NBLK * O * I + 2 * J * O + 4 * B * J * O
 
 STEPS = [("x", 0, 0, 8), ("w", 0), ("x", 1, 0, 8), ("w", 1), ("x", 2, 0, 8), ("w", 2), ("x", 3, 0, 8), ("w", 3), ("w", 4), ("w", 5), ("w", 6), ("w", 7), ("x", 4, 0, 8), ("x", 5, 0, 8), ("x", 6, 0, 8), ("x", 7, 0, 8)]
-PERM = {12: (2, 1), 13: (2, 1), 14: (2, 1), 15: (2, 1)}
+PERM = {12: (2, 2), 13: (2, 1), 14: (2, 1), 15: (3, 1)}
 AHEAD = 2
 LAG = 2
 HALF = 4

from contextlib import ExitStack

import concourse.mybir as mybir
from concourse.masks import make_identity

F32 = mybir.dt.float32
BF16 = mybir.dt.bfloat16
U32 = mybir.dt.uint32
U8 = mybir.dt.uint8
FP8X4 = mybir.dt.float8_e4m3fn_x4
ADD = mybir.AluOpType.add
MULT = mybir.AluOpType.mult

P = 128
B, J, I, O = 1024, 8, 512, 128
NT = B // P
NBLK = 3 * J - 2
FLOPS = 2 * B * O * I * NBLK
BYTES = 2 * B * J * I + 2 * 2 * NBLK * O * I + 2 * J * O + 4 * B * J * O

STEPS = [("x", 0, 0, 8), ("w", 0), ("x", 1, 0, 8), ("w", 1), ("x", 2, 0, 8), ("w", 2), ("x", 3, 0, 8), ("w", 3), ("w", 4), ("w", 5), ("w", 6), ("w", 7), ("x", 4, 0, 8), ("x", 5, 0, 8), ("x", 6, 0, 8), ("x", 7, 0, 8)]
PERM = {12: (2, 2), 13: (2, 1), 14: (2, 1), 15: (3, 1)}
AHEAD = 2
LAG = 2
HALF = 4


def neighbours(i):
    return list(range(max(i - 1, 0), min(i + 2, J)))


def tile_skeletonlinear_kernel(tc, x, weight, mask, bias, out):
    nc = tc.nc
    with ExitStack() as ctx:
        const = ctx.enter_context(tc.tile_pool(name="const", bufs=1))
        keep = ctx.enter_context(tc.tile_pool(name="keep", bufs=1))
        xraw = ctx.enter_context(tc.tile_pool(name="xraw", bufs=4))
        wraw = ctx.enter_context(tc.tile_pool(name="wraw", bufs=8))
        grp = ctx.enter_context(tc.tile_pool(name="grp", bufs=3))
        psum_t = ctx.enter_context(tc.psum_pool(name="psum_t", bufs=4))
        psum_a = ctx.enter_context(tc.psum_pool(name="psum_a", bufs=8 - 4))
        ctx.enter_context(tc.manual_schedule())

        x_view = x.rearrange("(t p) k -> p t k", p=P)
        out_view = out.rearrange("(t p) o -> p t o", p=P)

        ident = const.tile([P, P], F32, name="ident")
        make_identity(nc, ident[:])
        ones = const.tile([P, P], BF16, name="ones")
        nc.vector.memset(ones[:], 1.0)
        brow = const.tile([P, J * O], BF16, name="brow")
        nc.vector.memset(brow[:], 0.0)
        bias_bc = const.tile([P, J * O], F32, name="bias_bc")

        raw = {}
        msk = {}
        words = {}
        gt = {}
        xc = []
        xs = []
        wc = []
        ws = []
        for t in range(NT):
            cx = keep.tile([P, J * P], U32, name="xc%d" % t, align_bytes=64)
            sx = keep.tile([P, J * P], U8, name="xs%d" % t, align_bytes=64)
            xc.append(cx)
            xs.append(sx)
        for i in range(J):
            cw = keep.tile([P, len(neighbours(i)) * P], U32, name="wc%d" % i, align_bytes=64)
            sw = keep.tile([P, len(neighbours(i)) * P], U8, name="ws%d" % i, align_bytes=64)
            wc.append(cw)
            ws.append(sw)
        osb = keep.tile([P, NT, J * O], F32, name="osb")

        N = len(STEPS)
        runs = []
        last = {}
        for n in range(N):
            s = STEPS[n]
            if s[0] == "x":
                for b0 in range(0, s[3] - s[2], HALF):
                    runs.append((n, b0, min(HALF, s[3] - s[2] - b0)))
            else:
                runs.append((n, 0, len(neighbours(s[1]))))
            last[n] = len(runs) - 1
        R = len(runs)

        def blocks(n):
            s = STEPS[n]
            return len(neighbours(s[1])) if s[0] == "w" else s[3] - s[2]

        def load(n):
            s = STEPS[n]
            w = blocks(n) * I
            if s[0] == "x":
                raw[n] = xraw.tile([P, w], BF16, name="xr%d" % n, tag="xr")
                nc.sync.dma_start(out=raw[n][:], in_=x_view[:, s[1], s[2] * I:s[3] * I])
            else:
                i = s[1]
                lo = neighbours(i)[0] * I
                raw[n] = wraw.tile([P, w], BF16, name="wr%d" % n, tag="wr")
                msk[n] = wraw.tile([P, w], BF16, name="mr%d" % n, tag="mr")
                nc.sync.dma_start(out=raw[n][:], in_=weight[i * O:(i + 1) * O, lo:lo + w])
                nc.sync.dma_start(out=msk[n][:], in_=mask[i * O:(i + 1) * O, lo:lo + w])

        def bias_spread():
            for h in range(2):
                pb = psum_a.tile([P, 512], F32, name="pb", tag="acc")
                nc.tensor.matmul(out=pb[:], lhsT=ones[:], rhs=brow[:, 512 * h:512 * (h + 1)], start=True, stop=True)
                nc.scalar.copy(out=bias_bc[:, 512 * h:512 * (h + 1)], in_=pb[:])

        def stage_words(r):
            n, b0, nb = runs[r]
            s = STEPS[n]
            if s[0] == "w":
                wp = wraw.tile([P, nb * I], BF16, name="wp%d" % r, tag="wp", bufs=3)
                nc.vector.tensor_tensor(
                    out=wp[:].rearrange("p (u m e) -> p u m e", u=2, e=2),
                    in0=raw[n][:].rearrange("p (m u e) -> p u m e", u=2, e=2),
                    in1=msk[n][:].rearrange("p (m u e) -> p u m e", u=2, e=2),
                    op=MULT)
                words[r] = [(0, nb, wp[:].bitcast(F32).rearrange("p (u m) -> p u m", u=2))]
                return
            src = raw[n][:].bitcast(F32)[:, 256 * b0:256 * (b0 + nb)]
            dve, act = PERM.get(n, (0, 0))
            c1 = nb - act
            c0 = c1 - dve
            words[r] = [(0, c0, src.rearrange("p (m u) -> p u m", u=2))]
            if dve + act > 0:
                xp = xraw.tile([P, nb * I // 2], F32, name="xp%d" % r, tag="xp", bufs=3)
                for put, lo, hi in ((nc.vector.tensor_copy, c0, c1), (nc.scalar.copy, c1, nb)):
                    if hi > lo:
                        dst = xp[:, 256 * lo:256 * hi].rearrange("p (u m) -> p u m", u=2)
                        put(out=dst, in_=src[:, 256 * lo:256 * hi].rearrange("p (m u) -> p u m", u=2))
                        words[r].append((lo, hi, dst))

        def word_block(r, b, u):
            for lo, hi, view in words[r]:
                if lo <= b < hi:
                    return view[:, u, P * (b - lo):P * (b - lo + 1)]

        def stage_transpose(r):
            n, first, nb = runs[r]
            g = grp.tile([P, 4 * nb * P], BF16, name="g%d" % r, tag="gx" if STEPS[n][0] == "x" else "gw", align_bytes=64)
            g32 = g[:].bitcast(F32).rearrange("p (g r u) -> p g r u", r=P, u=2)
            for b0 in range(0, nb, 2):
                k = min(2, nb - b0)
                tp = psum_t.tile([P, 2, 2, P], F32, name="tp", tag="tp")
                for gg in range(k):
                    for u in range(2):
                        nc.tensor.transpose(out=tp[:, gg, u, :], in_=word_block(r, b0 + gg, u), identity=ident[:])
                put = nc.vector.tensor_copy if (r, b0) in () else nc.scalar.copy
                put(out=g32[:, b0:b0 + k, :, :], in_=tp[:, 0:k, :, :].rearrange("p g u r -> p g r u"))
            gt[r] = g

        def stage_quantise(r):
            n, first, nb = runs[r]
            s = STEPS[n]
            if s[0] == "x":
                codes, scales, c0 = xc[s[1]], xs[s[1]], s[2] + first
            else:
                codes, scales, c0 = wc[s[1]], ws[s[1]], 0
            b0 = 0
            for k in (4, 2, 1):
                while nb - b0 >= k:
                    lo, hi = P * (c0 + b0), P * (c0 + b0 + k)
                    nc.vector.quantize_mx(
                        out=codes[:, lo:hi].bitcast(FP8X4),
                        scales=scales[:, lo:hi],
                        in_=gt[r][:, 4 * P * b0:4 * P * (b0 + k)])
                    b0 = b0 + k

        def cell(acc_ap, t, i):
            ng = neighbours(i)
            for gi, g in enumerate(ng):
                nc.tensor.matmul_mx(
                    out=acc_ap,
                    lhsT=xc[t][:, P * g:P * (g + 1)].bitcast(FP8X4),
                    lhsT_scale=xs[t][:, P * g:P * (g + 1)],
                    rhs=wc[i][:, P * gi:P * (gi + 1)].bitcast(FP8X4),
                    rhs_scale=ws[i][:, P * gi:P * (gi + 1)],
                    start=(gi == 0),
                    stop=(gi == len(ng) - 1),
                )

        have_x = set()
        have_w = set()
        made = set()
        added = set()
        stored = set()
        queue = []
        accs = {}

        def ready(t, i):
            return i in have_w and (t, i) not in made and all((t, g) in have_x for g in neighbours(i))

        def open_cells(r):
            n, first, nb = runs[r]
            s = STEPS[n]
            if s[0] == "w":
                have_w.add(s[1])
                cells = [(t, s[1]) for t in range(NT) if ready(t, s[1])]
            else:
                for g in range(first, first + nb):
                    have_x.add((s[1], s[2] + g))
                cells = [(s[1], i) for i in range(J) if ready(s[1], i)]
                if r != last[n]:
                    cells = []
            for z in cells:
                made.add(z)
            for a in range(0, len(cells), 4):
                queue.append((r + LAG, n, cells[a:a + 4]))

        def stage_multiply(r):
            accs[r] = []
            count = 0
            while queue and queue[0][0] <= r and (count < 1 or STEPS[queue[0][1]][0] == "w" or r >= R):
                due, n, cells = queue.pop(0)
                acc = psum_a.tile([P, 4, O], F32, name="acc", tag="acc")
                for c, (t, i) in enumerate(cells):
                    cell(acc[:, c, :], t, i)
                accs[r].append((acc, n, cells))
                count = count + 1

        def stage_output(r):
            for acc, n, cells in accs[r]:
                t, i = cells[0]
                k = len(cells)
                if STEPS[n][0] == "w":
                    cols = slice(O * i, O * (i + 1))
                    nc.vector.tensor_tensor(
                        out=osb[:, t:t + k, cols],
                        in0=acc[:, 0:k, :],
                        in1=bias_bc[:, cols].unsqueeze(1).to_broadcast([P, k, O]),
                        op=ADD)
                else:
                    cols = slice(O * i, O * (i + k))
                    nc.vector.tensor_tensor(
                        out=osb[:, t, cols],
                        in0=acc[:, 0:k, :].rearrange("p c o -> p (c o)"),
                        in1=bias_bc[:, cols],
                        op=ADD)
                for z in cells:
                    added.add(z)
                if n >= N - 2:
                    nc.sync.dma_start(out=out_view[:, t, cols], in_=osb[:, t, cols])
                    for z in cells:
                        stored.add(z)
            for h in range(2):
                mine = range(4 * h, 4 * h + 4)
                ts = [t for t in range(NT) if all((t, i) in added and (t, i) not in stored for i in mine)]
                if len(ts) == 1 and h == 0 and ts[0] >= 4:
                    continue
                if len(ts) == 1 and h == 1 and (ts[0], 0) not in stored:
                    t = ts[0]
                    nc.sync.dma_start(out=out_view[:, t, :], in_=osb[:, t, :])
                    for i in range(J):
                        stored.add((t, i))
                    continue
                if ts:
                    cols = slice(512 * h, 512 * (h + 1))
                    nc.sync.dma_start(out=out_view[:, ts[0]:ts[-1] + 1, cols], in_=osb[:, ts[0]:ts[-1] + 1, cols])
                    for t in ts:
                        for i in mine:
                            stored.add((t, i))

        loaded = []

        def load_ahead(r):
            while len(loaded) < N:
                k = len(loaded)
                kind = STEPS[k][0]
                busy = [z for z in loaded if STEPS[z][0] == kind and last[z] >= r]
                if len(busy) >= (4 if kind == "x" else 8):
                    break
                load(k)
                loaded.append(k)
                if k == 0:
                    nc.sync.dma_start(out=brow[0:1, :], in_=bias.rearrange("(a n) -> a n", a=1))

        load_ahead(0)
        for r in range(AHEAD):
            stage_words(r)
        for r in range(R + LAG + 3):
            if 1 <= r <= R:
                stage_quantise(r - 1)
                open_cells(r - 1)
            if r < R:
                stage_transpose(r)
                load_ahead(r + 1)
                if r == 1:
                    bias_spread()
            stage_multiply(r)
            if r + AHEAD < R:
                stage_words(r + AHEAD)
            if r >= 1:
                stage_output(r - 1)
